import numpy as np
import ml_dtypes

BF16 = ml_dtypes.bfloat16


def bf(x):
    return np.asarray(x, np.float32).astype(BF16)


def f32(x):
    return np.asarray(x, np.float32)


def f64(x):
    return np.asarray(x).astype(np.float64)


def striped(idx):
    return np.tile(idx.reshape(-1, 16).T, (8, 1))


V, D, H, U, N = 2048, 128, 128, 512, 2048
P0 = (np.arange(D) % 2).astype(np.float64)[:, None]


def setup_inputs():
    return {"table": bf(np.random.standard_normal((D, V))), "v_w": bf(np.random.standard_normal((D, H)) / np.sqrt(D)), "v_b": f32(0.1 * np.random.standard_normal((H, 1))), "ff_w": bf(np.random.standard_normal((H, D)) / np.sqrt(H)), "ff_b": f32(0.1 * np.random.standard_normal((D, 1))), "head_w": bf(np.random.standard_normal((D, U)) / np.sqrt(D)), "head_b": f32(0.1 * np.random.standard_normal((U, 1))), "offs": striped(np.random.permutation(np.tile(np.arange(V), 2))[:N])}


def reference(table, v_w, v_b, ff_w, ff_b, head_w, head_b, offs):
    idx = offs[:16].T.reshape(-1)
    e = f64(table)[:, idx] + P0
    a = f64(v_w).T @ e + f64(v_b)
    r = f64(ff_w).T @ a + f64(ff_b)
    return f64(head_w).T @ r + f64(head_b)

@@ -1,0 +1,83 @@
+import concourse.mybir as mybir
+
+BF16, F32, I32, U16 = mybir.dt.bfloat16, mybir.dt.float32, mybir.dt.int32, mybir.dt.uint16
+
+P = 128
+V = 2048
+N = 2048
+U = 512
+PIECE = 512
+N_PIECES = N // PIECE
+U_BLOCKS = U // P
+
+FLOPS = 2 * N * (P * P + P * P + P * U)
+
+
+def tile_decodermodel_kernel(tc, table, v_w, v_b, ff_w, ff_b, head_w, head_b, offs, out):
+    nc = tc.nc
+    identity = mybir.ActivationFunctionType.Identity
+
+    with (
+        tc.tile_pool(name="held", bufs=1) as held,
+        tc.tile_pool(name="acts", bufs=N_PIECES) as acts,
+        tc.tile_pool(name="staged", bufs=8) as staged,
+        tc.psum_pool(name="banks", bufs=7) as banks,
+        tc.psum_pool(name="small", bufs=1) as small,
+    ):
+        offsets = held.tile([P, N // 16], U16, name="offsets")
+        nc.sync.dma_start(offsets[:], offs)
+        table_sb = held.tile([P, V], BF16)
+        nc.scalar.dma_start(table_sb[:], table)
+        v_w_sb = held.tile([P, P], BF16)
+        nc.sync.dma_start(v_w_sb[:], v_w)
+        ff_w_sb = held.tile([P, P], BF16)
+        nc.sync.dma_start(ff_w_sb[:], ff_w)
+        head_w_sb = held.tile([P, U], BF16)
+        nc.sync.dma_start(head_w_sb[:], head_w)
+        v_b_sb = held.tile([P, 1], F32)
+        nc.gpsimd.dma_start(v_b_sb[:], v_b)
+        ff_b_sb = held.tile([P, 1], F32)
+        nc.gpsimd.dma_start(ff_b_sb[:], ff_b)
+        head_b_sb = held.tile([P, U_BLOCKS], F32)
+        with nc.allow_non_contiguous_dma(reason="512 biases, one to a partition and block"):
+            nc.gpsimd.dma_start(head_b_sb[:], head_b.rearrange("(b p) one -> p (b one)", p=P))
+
+        row = held.tile([P, 1], I32)
+        nc.gpsimd.iota(row[:], pattern=[[0, 1]], base=0, channel_multiplier=1)
+        row_is_odd = held.tile([P, 1], I32)
+        nc.vector.tensor_single_scalar(row_is_odd[:], row[:], 1, op=mybir.AluOpType.bitwise_and)
+        position_code = held.tile([P, 1], BF16)
+        nc.vector.tensor_copy(position_code[:], row_is_odd[:])
+        code_share = small.tile([P, 1], F32)
+        nc.tensor.matmul(code_share[:], v_w_sb[:], position_code[:], start=True, stop=True)
+        a_bias = held.tile([P, 1], F32)
+        nc.vector.tensor_add(a_bias[:], code_share[:], v_b_sb[:])
+
+        def add_bias(turn, result, product, bias):
+            if turn % 2 == 0:
+                nc.vector.tensor_scalar_add(result, product, bias)
+            else:
+                nc.scalar.activation(result, product, identity, bias=bias)
+
+        a_sb = []
+        for k in range(N_PIECES):
+            a_ps = banks.tile([P, PIECE], F32, name="a_ps", tag="bank")
+            piece_offsets = offsets[:, k * (PIECE // 16) : (k + 1) * (PIECE // 16)]
+            nc.tensor.matmul(a_ps[:], v_w_sb[:], table_sb[:].indirect(piece_offsets), start=True, stop=True)
+            a_sb.append(acts.tile([P, PIECE], BF16, name="a_sb"))
+            add_bias(k, a_sb[k][:], a_ps[:], a_bias[:])
+
+        r_sb = []
+        for k in range(N_PIECES):
+            r_ps = banks.tile([P, PIECE], F32, name="r_ps", tag="bank")
+            nc.tensor.matmul(r_ps[:], ff_w_sb[:], a_sb[k][:], start=True, stop=True)
+            r_sb.append(acts.tile([P, PIECE], BF16, name="r_sb"))
+            add_bias(k, r_sb[k][:], r_ps[:], ff_b_sb[:])
+
+        for k in range(N_PIECES):
+            for b in range(U_BLOCKS):
+                out_ps = banks.tile([P, PIECE], F32, name="out_ps", tag="bank")
+                nc.tensor.matmul(out_ps[:], head_w_sb[:, b * P : (b + 1) * P], r_sb[k][:], start=True, stop=True)
+                logits = staged.tile([P, PIECE], F32)
+                add_bias(b, logits[:], out_ps[:], head_b_sb[:, b : b + 1])
+                nc.sync.dma_start(out[b * P : (b + 1) * P, k * PIECE : (k + 1) * PIECE], logits[:])

@@ -30,17 +30,17 @@ def tile_decodermodel_kernel(tc, table, v_w, v_b, ff_w, ff_b, head_w, head_b, of
         nc.scalar.dma_start(table_sb[:], table)
         v_w_sb = held.tile([P, P], BF16)
         nc.sync.dma_start(v_w_sb[:], v_w)
+        v_b_sb = held.tile([P, 1], F32)
+        nc.sync.dma_start(v_b_sb[:], v_b)
         ff_w_sb = held.tile([P, P], BF16)
         nc.sync.dma_start(ff_w_sb[:], ff_w)
-        head_w_sb = held.tile([P, U], BF16)
-        nc.sync.dma_start(head_w_sb[:], head_w)
-        v_b_sb = held.tile([P, 1], F32)
-        nc.gpsimd.dma_start(v_b_sb[:], v_b)
         ff_b_sb = held.tile([P, 1], F32)
-        nc.gpsimd.dma_start(ff_b_sb[:], ff_b)
+        nc.sync.dma_start(ff_b_sb[:], ff_b)
+        head_w_sb = held.tile([P, U], BF16)
+        nc.scalar.dma_start(head_w_sb[:], head_w)
         head_b_sb = held.tile([P, U_BLOCKS], F32)
         with nc.allow_non_contiguous_dma(reason="512 biases, one to a partition and block"):
-            nc.gpsimd.dma_start(head_b_sb[:], head_b.rearrange("(b p) one -> p (b one)", p=P))
+            nc.scalar.dma_start(head_b_sb[:], head_b.rearrange("(b p) one -> p (b one)", p=P))
 
         row = held.tile([P, 1], I32)
         nc.gpsimd.iota(row[:], pattern=[[0, 1]], base=0, channel_multiplier=1)

@@ -1,6 +1,6 @@
 import concourse.mybir as mybir
 
-BF16, F32, I32, U16 = mybir.dt.bfloat16, mybir.dt.float32, mybir.dt.int32, mybir.dt.uint16
+BF16, F32, U16 = mybir.dt.bfloat16, mybir.dt.float32, mybir.dt.uint16
 
 P = 128
 V = 2048
@@ -9,6 +9,7 @@ U = 512
 PIECE = 512
 N_PIECES = N // PIECE
 U_BLOCKS = U // P
+WARM_UPS = 5
 
 FLOPS = 2 * N * (P * P + P * P + P * U)
 
@@ -21,35 +22,44 @@ def tile_decodermodel_kernel(tc, table, v_w, v_b, ff_w, ff_b, head_w, head_b, of
         tc.tile_pool(name="held", bufs=1) as held,
         tc.tile_pool(name="acts", bufs=N_PIECES) as acts,
         tc.tile_pool(name="staged", bufs=8) as staged,
-        tc.psum_pool(name="banks", bufs=7) as banks,
+        tc.psum_pool(name="banks", bufs=6) as banks,
         tc.psum_pool(name="small", bufs=1) as small,
     ):
         offsets = held.tile([P, N // 16], U16, name="offsets")
         nc.sync.dma_start(offsets[:], offs)
         table_sb = held.tile([P, V], BF16)
-        nc.scalar.dma_start(table_sb[:], table)
+        nc.sync.dma_start(table_sb[:], table)
         v_w_sb = held.tile([P, P], BF16)
-        nc.sync.dma_start(v_w_sb[:], v_w)
+        nc.scalar.dma_start(v_w_sb[:], v_w)
         v_b_sb = held.tile([P, 1], F32)
-        nc.sync.dma_start(v_b_sb[:], v_b)
+        nc.scalar.dma_start(v_b_sb[:], v_b)
         ff_w_sb = held.tile([P, P], BF16)
-        nc.sync.dma_start(ff_w_sb[:], ff_w)
+        nc.scalar.dma_start(ff_w_sb[:], ff_w)
         ff_b_sb = held.tile([P, 1], F32)
-        nc.sync.dma_start(ff_b_sb[:], ff_b)
+        nc.scalar.dma_start(ff_b_sb[:], ff_b)
         head_w_sb = held.tile([P, U], BF16)
         nc.scalar.dma_start(head_w_sb[:], head_w)
         head_b_sb = held.tile([P, U_BLOCKS], F32)
         with nc.allow_non_contiguous_dma(reason="512 biases, one to a partition and block"):
             nc.scalar.dma_start(head_b_sb[:], head_b.rearrange("(b p) one -> p (b one)", p=P))
 
-        row = held.tile([P, 1], I32)
-        nc.gpsimd.iota(row[:], pattern=[[0, 1]], base=0, channel_multiplier=1)
-        row_is_odd = held.tile([P, 1], I32)
-        nc.vector.tensor_single_scalar(row_is_odd[:], row[:], 1, op=mybir.AluOpType.bitwise_and)
-        position_code = held.tile([P, 1], BF16)
-        nc.vector.tensor_copy(position_code[:], row_is_odd[:])
+        zeros = held.tile([P, PIECE], BF16)
+        nc.vector.memset(zeros[:], 0.0)
+        unread = small.tile([P, PIECE], F32)
+        for i in range(WARM_UPS):
+            nc.tensor.matmul(unread[:], zeros[:, 0:P], zeros[:], start=True, stop=True)
+
+        scratch = held.tile([P, 1], F32)
+        nc.scalar.activation(scratch[:], zeros[:, 0:1], identity)
+
+        stripes = held.tile([P, 32], BF16, align_bytes=64)
+        nc.vector.memset(stripes[:], 0.0)
+        nc.vector.memset(stripes[:].rearrange("p (k two) -> p k two", two=2)[:, :, 1:2], 1.0)
+        turned = held.tile([P, 32], BF16, align_bytes=64)
+        nc.vector.transpose(turned[:], stripes[:])
+        position_code = turned[:, 0:1]
         code_share = small.tile([P, 1], F32)
-        nc.tensor.matmul(code_share[:], v_w_sb[:], position_code[:], start=True, stop=True)
+        nc.tensor.matmul(code_share[:], v_w_sb[:], position_code, start=True, stop=True)
         a_bias = held.tile([P, 1], F32)
         nc.vector.tensor_add(a_bias[:], code_share[:], v_b_sb[:])
 

@@ -21,7 +21,7 @@ def tile_decodermodel_kernel(tc, table, v_w, v_b, ff_w, ff_b, head_w, head_b, of
     with (
         tc.tile_pool(name="held", bufs=1) as held,
         tc.tile_pool(name="acts", bufs=N_PIECES) as acts,
-        tc.tile_pool(name="staged", bufs=8) as staged,
+        tc.tile_pool(name="staged", bufs=U_BLOCKS) as staged,
         tc.psum_pool(name="banks", bufs=6) as banks,
         tc.psum_pool(name="small", bufs=1) as small,
     ):
@@ -77,17 +77,28 @@ def tile_decodermodel_kernel(tc, table, v_w, v_b, ff_w, ff_b, head_w, head_b, of
             a_sb.append(acts.tile([P, PIECE], BF16, name="a_sb"))
             add_bias(k, a_sb[k][:], a_ps[:], a_bias[:])
 
-        r_sb = []
-        for k in range(N_PIECES):
+        r_sb = [acts.tile([P, PIECE], BF16, name="r_sb") for k in range(N_PIECES)]
+
+        def feed(k):
             r_ps = banks.tile([P, PIECE], F32, name="r_ps", tag="bank")
             nc.tensor.matmul(r_ps[:], ff_w_sb[:], a_sb[k][:], start=True, stop=True)
-            r_sb.append(acts.tile([P, PIECE], BF16, name="r_sb"))
             add_bias(k, r_sb[k][:], r_ps[:], ff_b_sb[:])
 
-        for k in range(N_PIECES):
-            for b in range(U_BLOCKS):
-                out_ps = banks.tile([P, PIECE], F32, name="out_ps", tag="bank")
-                nc.tensor.matmul(out_ps[:], head_w_sb[:, b * P : (b + 1) * P], r_sb[k][:], start=True, stop=True)
-                logits = staged.tile([P, PIECE], F32)
-                add_bias(b, logits[:], out_ps[:], head_b_sb[:, b : b + 1])
-                nc.sync.dma_start(out[b * P : (b + 1) * P, k * PIECE : (k + 1) * PIECE], logits[:])
+        def head(turn, k, b, logits):
+            out_ps = banks.tile([P, PIECE], F32, name="out_ps", tag="bank")
+            nc.tensor.matmul(out_ps[:], head_w_sb[:, b * P : (b + 1) * P], r_sb[k][:], start=True, stop=True)
+            add_bias(turn, logits, out_ps[:], head_b_sb[:, b : b + 1])
+
+        feed(0)
+        for b in range(U_BLOCKS):
+            first = staged.tile([P, PIECE], F32, name="first")
+            head(b + 1, 0, b, first[:])
+            nc.sync.dma_start(out[b * P : (b + 1) * P, 0:PIECE], first[:])
+
+        for k in range(1, N_PIECES):
+            feed(k)
+        for b in range(U_BLOCKS):
+            rest = staged.tile([P, N - PIECE], F32, name="rest")
+            for k in range(1, N_PIECES):
+                head(b + k, k, b, rest[:, (k - 1) * PIECE : k * PIECE])
+            nc.sync.dma_start(out[b * P : (b + 1) * P, PIECE:N], rest[:])

@@ -7,6 +7,7 @@ V = 2048
 N = 2048
 U = 512
 PIECE = 512
+HALF = PIECE // 2
 N_PIECES = N // PIECE
 U_BLOCKS = U // P
 WARM_UPS = 5
@@ -20,7 +21,6 @@ def tile_decodermodel_kernel(tc, table, v_w, v_b, ff_w, ff_b, head_w, head_b, of
 
     with (
         tc.tile_pool(name="held", bufs=1) as held,
-        tc.tile_pool(name="acts", bufs=N_PIECES) as acts,
         tc.tile_pool(name="staged", bufs=U_BLOCKS) as staged,
         tc.psum_pool(name="banks", bufs=6) as banks,
         tc.psum_pool(name="small", bufs=1) as small,
@@ -28,15 +28,15 @@ def tile_decodermodel_kernel(tc, table, v_w, v_b, ff_w, ff_b, head_w, head_b, of
         offsets = held.tile([P, N // 16], U16, name="offsets")
         nc.sync.dma_start(offsets[:], offs)
         table_sb = held.tile([P, V], BF16)
-        nc.sync.dma_start(table_sb[:], table)
+        nc.scalar.dma_start(table_sb[:], table)
         v_w_sb = held.tile([P, P], BF16)
-        nc.scalar.dma_start(v_w_sb[:], v_w)
+        nc.sync.dma_start(v_w_sb[:], v_w)
         v_b_sb = held.tile([P, 1], F32)
-        nc.scalar.dma_start(v_b_sb[:], v_b)
+        nc.sync.dma_start(v_b_sb[:], v_b)
         ff_w_sb = held.tile([P, P], BF16)
-        nc.scalar.dma_start(ff_w_sb[:], ff_w)
+        nc.sync.dma_start(ff_w_sb[:], ff_w)
         ff_b_sb = held.tile([P, 1], F32)
-        nc.scalar.dma_start(ff_b_sb[:], ff_b)
+        nc.sync.dma_start(ff_b_sb[:], ff_b)
         head_w_sb = held.tile([P, U], BF16)
         nc.scalar.dma_start(head_w_sb[:], head_w)
         head_b_sb = held.tile([P, U_BLOCKS], F32)
@@ -69,36 +69,38 @@ def tile_decodermodel_kernel(tc, table, v_w, v_b, ff_w, ff_b, head_w, head_b, of
             else:
                 nc.scalar.activation(result, product, identity, bias=bias)
 
-        a_sb = []
+        a_sb = held.tile([P, N], BF16)
         for k in range(N_PIECES):
             a_ps = banks.tile([P, PIECE], F32, name="a_ps", tag="bank")
             piece_offsets = offsets[:, k * (PIECE // 16) : (k + 1) * (PIECE // 16)]
             nc.tensor.matmul(a_ps[:], v_w_sb[:], table_sb[:].indirect(piece_offsets), start=True, stop=True)
-            a_sb.append(acts.tile([P, PIECE], BF16, name="a_sb"))
-            add_bias(k, a_sb[k][:], a_ps[:], a_bias[:])
+            add_bias(k, a_sb[:, k * PIECE : (k + 1) * PIECE], a_ps[:], a_bias[:])
 
-        r_sb = [acts.tile([P, PIECE], BF16, name="r_sb") for k in range(N_PIECES)]
+        r_sb = held.tile([P, N], BF16)
 
-        def feed(k):
-            r_ps = banks.tile([P, PIECE], F32, name="r_ps", tag="bank")
-            nc.tensor.matmul(r_ps[:], ff_w_sb[:], a_sb[k][:], start=True, stop=True)
-            add_bias(k, r_sb[k][:], r_ps[:], ff_b_sb[:])
+        def feed(turn, lo, hi):
+            r_ps = banks.tile([P, hi - lo], F32, name="r_ps", tag="bank")
+            nc.tensor.matmul(r_ps[:], ff_w_sb[:], a_sb[:, lo:hi], start=True, stop=True)
+            add_bias(turn, r_sb[:, lo:hi], r_ps[:], ff_b_sb[:])
 
-        def head(turn, k, b, logits):
-            out_ps = banks.tile([P, PIECE], F32, name="out_ps", tag="bank")
-            nc.tensor.matmul(out_ps[:], head_w_sb[:, b * P : (b + 1) * P], r_sb[k][:], start=True, stop=True)
+        def head(turn, b, lo, hi, logits):
+            out_ps = banks.tile([P, hi - lo], F32, name="out_ps", tag="bank")
+            nc.tensor.matmul(out_ps[:], head_w_sb[:, b * P : (b + 1) * P], r_sb[:, lo:hi], start=True, stop=True)
             add_bias(turn, logits, out_ps[:], head_b_sb[:, b : b + 1])
 
-        feed(0)
+        feed(0, 0, HALF)
+        feed(1, HALF, PIECE)
         for b in range(U_BLOCKS):
             first = staged.tile([P, PIECE], F32, name="first")
-            head(b + 1, 0, b, first[:])
+            head(0, b, 0, HALF, first[:, 0:HALF])
+            head(1, b, HALF, PIECE, first[:, HALF:PIECE])
             nc.sync.dma_start(out[b * P : (b + 1) * P, 0:PIECE], first[:])
+            k = b + 1
+            if k < N_PIECES:
+                feed(k, k * PIECE, (k + 1) * PIECE)
 
-        for k in range(1, N_PIECES):
-            feed(k)
         for b in range(U_BLOCKS):
             rest = staged.tile([P, N - PIECE], F32, name="rest")
             for k in range(1, N_PIECES):
-                head(b + k, k, b, rest[:, (k - 1) * PIECE : k * PIECE])
+                head(b + k, b, k * PIECE, (k + 1) * PIECE, rest[:, (k - 1) * PIECE : k * PIECE])
             nc.sync.dma_start(out[b * P : (b + 1) * P, PIECE:N], rest[:])

@@ -10,7 +10,6 @@ PIECE = 512
 HALF = PIECE // 2
 N_PIECES = N // PIECE
 U_BLOCKS = U // P
-WARM_UPS = 5
 
 FLOPS = 2 * N * (P * P + P * P + P * U)
 
@@ -22,7 +21,7 @@ def tile_decodermodel_kernel(tc, table, v_w, v_b, ff_w, ff_b, head_w, head_b, of
     with (
         tc.tile_pool(name="held", bufs=1) as held,
         tc.tile_pool(name="staged", bufs=U_BLOCKS) as staged,
-        tc.psum_pool(name="banks", bufs=6) as banks,
+        tc.psum_pool(name="banks", bufs=7) as banks,
         tc.psum_pool(name="small", bufs=1) as small,
     ):
         offsets = held.tile([P, N // 16], U16, name="offsets")
@@ -43,21 +42,16 @@ def tile_decodermodel_kernel(tc, table, v_w, v_b, ff_w, ff_b, head_w, head_b, of
         with nc.allow_non_contiguous_dma(reason="512 biases, one to a partition and block"):
             nc.scalar.dma_start(head_b_sb[:], head_b.rearrange("(b p) one -> p (b one)", p=P))
 
-        zeros = held.tile([P, PIECE], BF16)
-        nc.vector.memset(zeros[:], 0.0)
-        unread = small.tile([P, PIECE], F32)
-        for i in range(WARM_UPS):
-            nc.tensor.matmul(unread[:], zeros[:, 0:P], zeros[:], start=True, stop=True)
-
-        scratch = held.tile([P, 1], F32)
-        nc.scalar.activation(scratch[:], zeros[:, 0:1], identity)
-
         stripes = held.tile([P, 32], BF16, align_bytes=64)
         nc.vector.memset(stripes[:], 0.0)
         nc.vector.memset(stripes[:].rearrange("p (k two) -> p k two", two=2)[:, :, 1:2], 1.0)
         turned = held.tile([P, 32], BF16, align_bytes=64)
         nc.vector.transpose(turned[:], stripes[:])
         position_code = turned[:, 0:1]
+
+        scratch = held.tile([P, 1], F32)
+        nc.scalar.activation(scratch[:], position_code, identity)
+
         code_share = small.tile([P, 1], F32)
         nc.tensor.matmul(code_share[:], v_w_sb[:], position_code, start=True, stop=True)
         a_bias = held.tile([P, 1], F32)

@@ -57,44 +57,49 @@ def tile_decodermodel_kernel(tc, table, v_w, v_b, ff_w, ff_b, head_w, head_b, of
         a_bias = held.tile([P, 1], F32)
         nc.vector.tensor_add(a_bias[:], code_share[:], v_b_sb[:])
 
-        def add_bias(turn, result, product, bias):
-            if turn % 2 == 0:
+        evacuated = []
+
+        def add_bias(result, product, bias):
+            if len(evacuated) % 2 == 0:
                 nc.vector.tensor_scalar_add(result, product, bias)
             else:
                 nc.scalar.activation(result, product, identity, bias=bias)
+            evacuated.append(result)
 
         a_sb = held.tile([P, N], BF16)
-        for k in range(N_PIECES):
-            a_ps = banks.tile([P, PIECE], F32, name="a_ps", tag="bank")
-            piece_offsets = offsets[:, k * (PIECE // 16) : (k + 1) * (PIECE // 16)]
-            nc.tensor.matmul(a_ps[:], v_w_sb[:], table_sb[:].indirect(piece_offsets), start=True, stop=True)
-            add_bias(k, a_sb[:, k * PIECE : (k + 1) * PIECE], a_ps[:], a_bias[:])
+        lo = 0
+        for width in (PIECE,) * (N_PIECES - 1) + (HALF, HALF):
+            a_ps = banks.tile([P, width], F32, name="a_ps", tag="bank")
+            some_offsets = offsets[:, lo // 16 : (lo + width) // 16]
+            nc.tensor.matmul(a_ps[:], v_w_sb[:], table_sb[:].indirect(some_offsets), start=True, stop=True)
+            add_bias(a_sb[:, lo : lo + width], a_ps[:], a_bias[:])
+            lo += width
 
         r_sb = held.tile([P, N], BF16)
 
-        def feed(turn, lo, hi):
+        def feed(lo, hi):
             r_ps = banks.tile([P, hi - lo], F32, name="r_ps", tag="bank")
             nc.tensor.matmul(r_ps[:], ff_w_sb[:], a_sb[:, lo:hi], start=True, stop=True)
-            add_bias(turn, r_sb[:, lo:hi], r_ps[:], ff_b_sb[:])
+            add_bias(r_sb[:, lo:hi], r_ps[:], ff_b_sb[:])
 
-        def head(turn, b, lo, hi, logits):
+        def head(b, lo, hi, logits):
             out_ps = banks.tile([P, hi - lo], F32, name="out_ps", tag="bank")
             nc.tensor.matmul(out_ps[:], head_w_sb[:, b * P : (b + 1) * P], r_sb[:, lo:hi], start=True, stop=True)
-            add_bias(turn, logits, out_ps[:], head_b_sb[:, b : b + 1])
+            add_bias(logits, out_ps[:], head_b_sb[:, b : b + 1])
 
-        feed(0, 0, HALF)
-        feed(1, HALF, PIECE)
+        feed(0, HALF)
+        feed(HALF, PIECE)
         for b in range(U_BLOCKS):
             first = staged.tile([P, PIECE], F32, name="first")
-            head(0, b, 0, HALF, first[:, 0:HALF])
-            head(1, b, HALF, PIECE, first[:, HALF:PIECE])
+            head(b, 0, HALF, first[:, 0:HALF])
+            head(b, HALF, PIECE, first[:, HALF:PIECE])
             nc.sync.dma_start(out[b * P : (b + 1) * P, 0:PIECE], first[:])
             k = b + 1
             if k < N_PIECES:
-                feed(k, k * PIECE, (k + 1) * PIECE)
+                feed(k * PIECE, (k + 1) * PIECE)
 
         for b in range(U_BLOCKS):
             rest = staged.tile([P, N - PIECE], F32, name="rest")
             for k in range(1, N_PIECES):
-                head(b + k, b, k * PIECE, (k + 1) * PIECE, rest[:, (k - 1) * PIECE : k * PIECE])
+                head(b, k * PIECE, (k + 1) * PIECE, rest[:, (k - 1) * PIECE : k * PIECE])
             nc.sync.dma_start(out[b * P : (b + 1) * P, PIECE:N], rest[:])

@@ -89,12 +89,16 @@ def tile_decodermodel_kernel(tc, table, v_w, v_b, ff_w, ff_b, head_w, head_b, of
 
         feed(0, HALF)
         feed(HALF, PIECE)
+        feed(PIECE, 2 * PIECE)
         for b in range(U_BLOCKS):
             first = staged.tile([P, PIECE], F32, name="first")
-            head(b, 0, HALF, first[:, 0:HALF])
-            head(b, HALF, PIECE, first[:, HALF:PIECE])
+            if b == 0:
+                head(b, 0, HALF, first[:, 0:HALF])
+                head(b, HALF, PIECE, first[:, HALF:PIECE])
+            else:
+                head(b, 0, PIECE, first[:])
             nc.sync.dma_start(out[b * P : (b + 1) * P, 0:PIECE], first[:])
-            k = b + 1
+            k = b + 2
             if k < N_PIECES:
                 feed(k * PIECE, (k + 1) * PIECE)
 

@@ -24,12 +24,12 @@ def tile_decodermodel_kernel(tc, table, v_w, v_b, ff_w, ff_b, head_w, head_b, of
         tc.psum_pool(name="banks", bufs=7) as banks,
         tc.psum_pool(name="small", bufs=1) as small,
     ):
+        table_sb = held.tile([P, V], BF16)
+        nc.sync.dma_start(table_sb[:], table)
         offsets = held.tile([P, N // 16], U16, name="offsets")
         nc.sync.dma_start(offsets[:], offs)
-        table_sb = held.tile([P, V], BF16)
-        nc.scalar.dma_start(table_sb[:], table)
         v_w_sb = held.tile([P, P], BF16)
-        nc.sync.dma_start(v_w_sb[:], v_w)
+        nc.scalar.dma_start(v_w_sb[:], v_w)
         v_b_sb = held.tile([P, 1], F32)
         nc.sync.dma_start(v_b_sb[:], v_b)
         ff_w_sb = held.tile([P, P], BF16)

@@ -37,10 +37,10 @@ def tile_decodermodel_kernel(tc, table, v_w, v_b, ff_w, ff_b, head_w, head_b, of
         ff_b_sb = held.tile([P, 1], F32)
         nc.sync.dma_start(ff_b_sb[:], ff_b)
         head_w_sb = held.tile([P, U], BF16)
-        nc.scalar.dma_start(head_w_sb[:], head_w)
+        nc.sync.dma_start(head_w_sb[:], head_w)
         head_b_sb = held.tile([P, U_BLOCKS], F32)
         with nc.allow_non_contiguous_dma(reason="512 biases, one to a partition and block"):
-            nc.scalar.dma_start(head_b_sb[:], head_b.rearrange("(b p) one -> p (b one)", p=P))
+            nc.sync.dma_start(head_b_sb[:], head_b.rearrange("(b p) one -> p (b one)", p=P))
 
         stripes = held.tile([P, 32], BF16, align_bytes=64)
         nc.vector.memset(stripes[:], 0.0)

@@ -6,9 +6,9 @@ P = 128
 V = 2048
 N = 2048
 U = 512
-PIECE = 512
-HALF = PIECE // 2
-N_PIECES = N // PIECE
+FIRST = 576
+QUARTER, HALF = FIRST // 4, FIRST // 2
+WIDTH = 320
 U_BLOCKS = U // P
 
 FLOPS = 2 * N * (P * P + P * P + P * U)
@@ -66,14 +66,17 @@ def tile_decodermodel_kernel(tc, table, v_w, v_b, ff_w, ff_b, head_w, head_b, of
                 nc.scalar.activation(result, product, identity, bias=bias)
             evacuated.append(result)
 
+        def cut(lo, hi, width):
+            return [(x, min(x + width, hi)) for x in range(lo, hi, width)]
+
+        rest_runs = cut(FIRST, N, WIDTH)
+
         a_sb = held.tile([P, N], BF16)
-        lo = 0
-        for width in (PIECE,) * (N_PIECES - 1) + (HALF, HALF):
-            a_ps = banks.tile([P, width], F32, name="a_ps", tag="bank")
-            some_offsets = offsets[:, lo // 16 : (lo + width) // 16]
+        for lo, hi in cut(0, FIRST, HALF) + rest_runs:
+            a_ps = banks.tile([P, hi - lo], F32, name="a_ps", tag="bank")
+            some_offsets = offsets[:, lo // 16 : hi // 16]
             nc.tensor.matmul(a_ps[:], v_w_sb[:], table_sb[:].indirect(some_offsets), start=True, stop=True)
-            add_bias(a_sb[:, lo : lo + width], a_ps[:], a_bias[:])
-            lo += width
+            add_bias(a_sb[:, lo:hi], a_ps[:], a_bias[:])
 
         r_sb = held.tile([P, N], BF16)
 
@@ -87,23 +90,19 @@ def tile_decodermodel_kernel(tc, table, v_w, v_b, ff_w, ff_b, head_w, head_b, of
             nc.tensor.matmul(out_ps[:], head_w_sb[:, b * P : (b + 1) * P], r_sb[:, lo:hi], start=True, stop=True)
             add_bias(logits, out_ps[:], head_b_sb[:, b : b + 1])
 
-        feed(0, HALF)
-        feed(HALF, PIECE)
-        feed(PIECE, 2 * PIECE)
+        for lo, hi in cut(0, FIRST, QUARTER):
+            feed(lo, hi)
         for b in range(U_BLOCKS):
-            first = staged.tile([P, PIECE], F32, name="first")
-            if b == 0:
-                head(b, 0, HALF, first[:, 0:HALF])
-                head(b, HALF, PIECE, first[:, HALF:PIECE])
-            else:
-                head(b, 0, PIECE, first[:])
-            nc.sync.dma_start(out[b * P : (b + 1) * P, 0:PIECE], first[:])
-            k = b + 2
-            if k < N_PIECES:
-                feed(k * PIECE, (k + 1) * PIECE)
+            feed(*rest_runs[b])
+            first = staged.tile([P, FIRST], F32, name="first")
+            for lo, hi in cut(0, FIRST, QUARTER if b == 0 else HALF):
+                head(b, lo, hi, first[:, lo:hi])
+            nc.sync.dma_start(out[b * P : (b + 1) * P, 0:FIRST], first[:])
+        for lo, hi in rest_runs[U_BLOCKS:]:
+            feed(lo, hi)
 
         for b in range(U_BLOCKS):
-            rest = staged.tile([P, N - PIECE], F32, name="rest")
-            for k in range(1, N_PIECES):
-                head(b, k * PIECE, (k + 1) * PIECE, rest[:, (k - 1) * PIECE : k * PIECE])
-            nc.sync.dma_start(out[b * P : (b + 1) * P, PIECE:N], rest[:])
+            rest = staged.tile([P, N - FIRST], F32, name="rest")
+            for lo, hi in rest_runs:
+                head(b, lo, hi, rest[:, lo - FIRST : hi - FIRST])
+            nc.sync.dma_start(out[b * P : (b + 1) * P, FIRST:N], rest[:])

@@ -105,4 +105,5 @@ def tile_decodermodel_kernel(tc, table, v_w, v_b, ff_w, ff_b, head_w, head_b, of
             rest = staged.tile([P, N - FIRST], F32, name="rest")
             for lo, hi in rest_runs:
                 head(b, lo, hi, rest[:, lo - FIRST : hi - FIRST])
-            nc.sync.dma_start(out[b * P : (b + 1) * P, FIRST:N], rest[:])
+            queue = nc.sync if b % 2 == 0 else nc.scalar
+            queue.dma_start(out[b * P : (b + 1) * P, FIRST:N], rest[:])

@@ -21,8 +21,7 @@ def tile_decodermodel_kernel(tc, table, v_w, v_b, ff_w, ff_b, head_w, head_b, of
     with (
         tc.tile_pool(name="held", bufs=1) as held,
         tc.tile_pool(name="staged", bufs=U_BLOCKS) as staged,
-        tc.psum_pool(name="banks", bufs=7) as banks,
-        tc.psum_pool(name="small", bufs=1) as small,
+        tc.psum_pool(name="banks", bufs=8) as banks,
     ):
         table_sb = held.tile([P, V], BF16)
         nc.sync.dma_start(table_sb[:], table)
@@ -52,7 +51,7 @@ def tile_decodermodel_kernel(tc, table, v_w, v_b, ff_w, ff_b, head_w, head_b, of
         scratch = held.tile([P, 1], F32)
         nc.scalar.activation(scratch[:], position_code, identity)
 
-        code_share = small.tile([P, 1], F32)
+        code_share = banks.tile([P, 1], F32, name="code_share", tag="bank")
         nc.tensor.matmul(code_share[:], v_w_sb[:], position_code, start=True, stop=True)
         a_bias = held.tile([P, 1], F32)
         nc.vector.tensor_add(a_bias[:], code_share[:], v_b_sb[:])
@@ -65,6 +64,14 @@ def tile_decodermodel_kernel(tc, table, v_w, v_b, ff_w, ff_b, head_w, head_b, of
             else:
                 nc.scalar.activation(result, product, identity, bias=bias)
             evacuated.append(result)
+
+        stored = []
+
+        def store(where, tile):
+            scalar_was_last = len(evacuated) % 2 == 0
+            queue = nc.scalar if stored and scalar_was_last else nc.sync
+            queue.dma_start(where, tile)
+            stored.append(where)
 
         def cut(lo, hi, width):
             return [(x, min(x + width, hi)) for x in range(lo, hi, width)]
@@ -97,7 +104,7 @@ def tile_decodermodel_kernel(tc, table, v_w, v_b, ff_w, ff_b, head_w, head_b, of
             first = staged.tile([P, FIRST], F32, name="first")
             for lo, hi in cut(0, FIRST, QUARTER if b == 0 else HALF):
                 head(b, lo, hi, first[:, lo:hi])
-            nc.sync.dma_start(out[b * P : (b + 1) * P, 0:FIRST], first[:])
+            store(out[b * P : (b + 1) * P, 0:FIRST], first[:])
         for lo, hi in rest_runs[U_BLOCKS:]:
             feed(lo, hi)
 
@@ -105,5 +112,4 @@ def tile_decodermodel_kernel(tc, table, v_w, v_b, ff_w, ff_b, head_w, head_b, of
             rest = staged.tile([P, N - FIRST], F32, name="rest")
             for lo, hi in rest_runs:
                 head(b, lo, hi, rest[:, lo - FIRST : hi - FIRST])
-            queue = nc.sync if b % 2 == 0 else nc.scalar
-            queue.dma_start(out[b * P : (b + 1) * P, FIRST:N], rest[:])
+            store(out[b * P : (b + 1) * P, FIRST:N], rest[:])

@@ -23,7 +23,7 @@ def tile_decodermodel_kernel(tc, table, v_w, v_b, ff_w, ff_b, head_w, head_b, of
         tc.tile_pool(name="staged", bufs=U_BLOCKS) as staged,
         tc.psum_pool(name="banks", bufs=8) as banks,
     ):
-        table_sb = held.tile([P, V], BF16)
+        table_sb = held.tile([P, V], BF16, align_bytes=256)
         nc.sync.dma_start(table_sb[:], table)
         offsets = held.tile([P, N // 16], U16, name="offsets")
         nc.sync.dma_start(offsets[:], offs)
@@ -97,11 +97,12 @@ def tile_decodermodel_kernel(tc, table, v_w, v_b, ff_w, ff_b, head_w, head_b, of
             nc.tensor.matmul(out_ps[:], head_w_sb[:, b * P : (b + 1) * P], r_sb[:, lo:hi], start=True, stop=True)
             add_bias(logits, out_ps[:], head_b_sb[:, b : b + 1])
 
+
         for lo, hi in cut(0, FIRST, QUARTER):
             feed(lo, hi)
         for b in range(U_BLOCKS):
             feed(*rest_runs[b])
-            first = staged.tile([P, FIRST], F32, name="first")
+            first = staged.tile([P, FIRST], F32, name="first", align_bytes=256)
             for lo, hi in cut(0, FIRST, QUARTER if b == 0 else HALF):
                 head(b, lo, hi, first[:, lo:hi])
             store(out[b * P : (b + 1) * P, 0:FIRST], first[:])
@@ -109,7 +110,7 @@ def tile_decodermodel_kernel(tc, table, v_w, v_b, ff_w, ff_b, head_w, head_b, of
             feed(lo, hi)
 
         for b in range(U_BLOCKS):
-            rest = staged.tile([P, N - FIRST], F32, name="rest")
+            rest = staged.tile([P, N - FIRST], F32, name="rest", align_bytes=256)
             for lo, hi in rest_runs:
                 head(b, lo, hi, rest[:, lo - FIRST : hi - FIRST])
             store(out[b * P : (b + 1) * P, FIRST:N], rest[:])

@@ -9,6 +9,7 @@ U = 512
 FIRST = 576
 QUARTER, HALF = FIRST // 4, FIRST // 2
 WIDTH = 320
+LAG = 2
 U_BLOCKS = U // P
 
 FLOPS = 2 * N * (P * P + P * P + P * U)
@@ -100,17 +101,21 @@ def tile_decodermodel_kernel(tc, table, v_w, v_b, ff_w, ff_b, head_w, head_b, of
 
         for lo, hi in cut(0, FIRST, QUARTER):
             feed(lo, hi)
+        left = []
         for b in range(U_BLOCKS):
-            feed(*rest_runs[b])
-            first = staged.tile([P, FIRST], F32, name="first", align_bytes=256)
-            for lo, hi in cut(0, FIRST, QUARTER if b == 0 else HALF):
-                head(b, lo, hi, first[:, lo:hi])
-            store(out[b * P : (b + 1) * P, 0:FIRST], first[:])
-        for lo, hi in rest_runs[U_BLOCKS:]:
+            if b < U_BLOCKS - LAG:
+                feed(*rest_runs[b])
+            runs = cut(0, FIRST, QUARTER if b == 0 else HALF) + rest_runs[: max(b + 1 - LAG, 0)]
+            left.append(runs[-1][1])
+            early = staged.tile([P, left[b]], F32, name="early", align_bytes=256)
+            for lo, hi in runs:
+                head(b, lo, hi, early[:, lo:hi])
+            store(out[b * P : (b + 1) * P, 0 : left[b]], early[:])
+        for lo, hi in rest_runs[U_BLOCKS - LAG :]:
             feed(lo, hi)
 
         for b in range(U_BLOCKS):
-            rest = staged.tile([P, N - FIRST], F32, name="rest", align_bytes=256)
-            for lo, hi in rest_runs:
-                head(b, lo, hi, rest[:, lo - FIRST : hi - FIRST])
-            store(out[b * P : (b + 1) * P, FIRST:N], rest[:])
+            late = staged.tile([P, N - left[b]], F32, name="late", align_bytes=256)
+            for lo, hi in rest_runs[max(b + 1 - LAG, 0) :]:
+                head(b, lo, hi, late[:, lo - left[b] : hi - left[b]])
+            store(out[b * P : (b + 1) * P, left[b] : N], late[:])

import concourse.mybir as mybir

BF16, F32, U16 = mybir.dt.bfloat16, mybir.dt.float32, mybir.dt.uint16

P = 128
V = 2048
N = 2048
U = 512
FIRST = 576
QUARTER, HALF = FIRST // 4, FIRST // 2
WIDTH = 320
LAG = 2
U_BLOCKS = U // P

FLOPS = 2 * N * (P * P + P * P + P * U)


def tile_decodermodel_kernel(tc, table, v_w, v_b, ff_w, ff_b, head_w, head_b, offs, out):
    nc = tc.nc
    identity = mybir.ActivationFunctionType.Identity

    with (
        tc.tile_pool(name="held", bufs=1) as held,
        tc.tile_pool(name="staged", bufs=U_BLOCKS) as staged,
        tc.psum_pool(name="banks", bufs=8) as banks,
    ):
        table_sb = held.tile([P, V], BF16, align_bytes=256)
        nc.sync.dma_start(table_sb[:], table)
        offsets = held.tile([P, N // 16], U16, name="offsets")
        nc.sync.dma_start(offsets[:], offs)
        v_w_sb = held.tile([P, P], BF16)
        nc.scalar.dma_start(v_w_sb[:], v_w)
        v_b_sb = held.tile([P, 1], F32)
        nc.sync.dma_start(v_b_sb[:], v_b)
        ff_w_sb = held.tile([P, P], BF16)
        nc.sync.dma_start(ff_w_sb[:], ff_w)
        ff_b_sb = held.tile([P, 1], F32)
        nc.sync.dma_start(ff_b_sb[:], ff_b)
        head_w_sb = held.tile([P, U], BF16)
        nc.sync.dma_start(head_w_sb[:], head_w)
        head_b_sb = held.tile([P, U_BLOCKS], F32)
        with nc.allow_non_contiguous_dma(reason="512 biases, one to a partition and block"):
            nc.sync.dma_start(head_b_sb[:], head_b.rearrange("(b p) one -> p (b one)", p=P))

        stripes = held.tile([P, 32], BF16, align_bytes=64)
        nc.vector.memset(stripes[:], 0.0)
        nc.vector.memset(stripes[:].rearrange("p (k two) -> p k two", two=2)[:, :, 1:2], 1.0)
        turned = held.tile([P, 32], BF16, align_bytes=64)
        nc.vector.transpose(turned[:], stripes[:])
        position_code = turned[:, 0:1]

        scratch = held.tile([P, 1], F32)
        nc.scalar.activation(scratch[:], position_code, identity)

        code_share = banks.tile([P, 1], F32, name="code_share", tag="bank")
        nc.tensor.matmul(code_share[:], v_w_sb[:], position_code, start=True, stop=True)
        a_bias = held.tile([P, 1], F32)
        nc.vector.tensor_add(a_bias[:], code_share[:], v_b_sb[:])

        evacuated = []

        def add_bias(result, product, bias):
            if len(evacuated) % 2 == 0:
                nc.vector.tensor_scalar_add(result, product, bias)
            else:
                nc.scalar.activation(result, product, identity, bias=bias)
            evacuated.append(result)

        stored = []

        def store(where, tile):
            scalar_was_last = len(evacuated) % 2 == 0
            queue = nc.scalar if stored and scalar_was_last else nc.sync
            queue.dma_start(where, tile)
            stored.append(where)

        def cut(lo, hi, width):
            return [(x, min(x + width, hi)) for x in range(lo, hi, width)]

        rest_runs = cut(FIRST, N, WIDTH)

        a_sb = held.tile([P, N], BF16)
        for lo, hi in cut(0, FIRST, HALF) + rest_runs:
            a_ps = banks.tile([P, hi - lo], F32, name="a_ps", tag="bank")
            some_offsets = offsets[:, lo // 16 : hi // 16]
            nc.tensor.matmul(a_ps[:], v_w_sb[:], table_sb[:].indirect(some_offsets), start=True, stop=True)
            add_bias(a_sb[:, lo:hi], a_ps[:], a_bias[:])

        r_sb = held.tile([P, N], BF16)

        def feed(lo, hi):
            r_ps = banks.tile([P, hi - lo], F32, name="r_ps", tag="bank")
            nc.tensor.matmul(r_ps[:], ff_w_sb[:], a_sb[:, lo:hi], start=True, stop=True)
            add_bias(r_sb[:, lo:hi], r_ps[:], ff_b_sb[:])

        def head(b, lo, hi, logits):
            out_ps = banks.tile([P, hi - lo], F32, name="out_ps", tag="bank")
            nc.tensor.matmul(out_ps[:], head_w_sb[:, b * P : (b + 1) * P], r_sb[:, lo:hi], start=True, stop=True)
            add_bias(logits, out_ps[:], head_b_sb[:, b : b + 1])


        for lo, hi in cut(0, FIRST, QUARTER):
            feed(lo, hi)
        left = []
        for b in range(U_BLOCKS):
            if b < U_BLOCKS - LAG:
                feed(*rest_runs[b])
            runs = cut(0, FIRST, QUARTER if b == 0 else HALF) + rest_runs[: max(b + 1 - LAG, 0)]
            left.append(runs[-1][1])
            early = staged.tile([P, left[b]], F32, name="early", align_bytes=256)
            for lo, hi in runs:
                head(b, lo, hi, early[:, lo:hi])
            store(out[b * P : (b + 1) * P, 0 : left[b]], early[:])
        for lo, hi in rest_runs[U_BLOCKS - LAG :]:
            feed(lo, hi)

        for b in range(U_BLOCKS):
            late = staged.tile([P, N - left[b]], F32, name="late", align_bytes=256)
            for lo, hi in rest_runs[max(b + 1 - LAG, 0) :]:
                head(b, lo, hi, late[:, lo - left[b] : hi - left[b]])
            store(out[b * P : (b + 1) * P, left[b] : N], late[:])
